import numpy as np
import ml_dtypes


def mxq(x, axis, fmt="e4m3"):
    dtype, down = {"e4m3": (ml_dtypes.float8_e4m3fn, 7), "e5m2": (ml_dtypes.float8_e5m2, 14)}[fmt]
    v = np.moveaxis(np.asarray(x, np.float32).astype(ml_dtypes.bfloat16).astype(np.float64), axis, -1)
    blocks = v.reshape(v.shape[:-1] + (-1, 32))
    amax = np.abs(blocks).max(-1, keepdims=True)
    byte = np.maximum(np.where(amax > 0, np.frexp(amax)[1] - 1 + 127, 0) - down, 1)
    scale = np.exp2(byte - 127.0)
    codes = (blocks / scale).astype(np.float32).astype(dtype).astype(np.float64)
    return np.moveaxis((codes * scale).reshape(v.shape), -1, axis)


WIDE = False


def mx_kscale(k):
    if not WIDE:
        return np.ones(k)
    levels = np.array([10, -10, 5, -5, 0])
    a = np.random.permutation(np.resize(levels, k // 512 * 4)).reshape(k // 512, 4)
    idx = np.arange(k)
    return np.exp2(a[idx // 512, idx % 128 // 32])


BF16 = ml_dtypes.bfloat16


def bf(x):
    return np.asarray(x, np.float32).astype(BF16)


def f64(x):
    return np.asarray(x).astype(np.float64)


B, C, H, W = 1, 1024, 32, 32
C2 = C // 2
N = H * W


def sigmoid(v):
    return 1.0 / (1.0 + np.exp(-v))


def setup_inputs():
    t = mx_kscale(C2)
    v2 = np.random.standard_normal((B, C2, N)) * 6.0 / np.sqrt(N) + np.random.standard_normal((1, C2, 1)) * 6.0 / N
    return {
        'q2': bf(np.random.standard_normal((B, N)) * 0.8),
        'k1': bf(1.0 + 2.5 * np.random.random((B, N))),
        'v2': bf(v2 * t[None, :, None]),
        'wc1': bf(np.random.standard_normal((C, C2)) * 0.25 / np.sqrt(C2) / t[None, :]),
        'bc1': bf(np.random.standard_normal(C) * 0.3),
        'gamma2': bf(0.7 + 0.1 * np.random.standard_normal(1)),
        'x2': bf(np.random.standard_normal((B, C, H, W))),
    }


def reference(q2, k1, v2, wc1, bc1, gamma2, x2):
    att1 = sigmoid(f64(q2)[:, :, None] * f64(k1)[:, None, :])
    agg = mxq(f64(v2), 2, 'e4m3') @ mxq(att1, 2, 'e4m3').transpose(0, 2, 1)
    y = (mxq(f64(wc1), 1, 'e4m3') @ mxq(agg, 1, 'e4m3')) + f64(bc1)[None, :, None]
    return f64(x2) + f64(gamma2)[0] * y.reshape(B, C, H, W)

@@ -1,0 +1,211 @@
+from contextlib import ExitStack
+
+from concourse import mybir
+from concourse.masks import make_identity
+
+F32 = mybir.dt.float32
+BF16 = mybir.dt.bfloat16
+U32 = mybir.dt.uint32
+U8 = mybir.dt.uint8
+FP8X4 = mybir.dt.float8_e4m3fn_x4
+ACT = mybir.ActivationFunctionType
+ALU = mybir.AluOpType
+
+P = 128
+PACK = 4
+PIX = 1024
+C_IN = 512
+C_OUT = 1024
+K_PASSES = PIX // (P * PACK)
+C_TILES = C_IN // P
+O_TILES = C_OUT // P
+BANK = 512
+M_CHUNK = 256
+M_SUB = BANK // C_TILES
+
+FLOPS = 2 * C_IN * PIX * PIX + 2 * C_OUT * C_IN * PIX
+
+
+def word_view(grouped):
+    flat = grouped.rearrange("p c t -> p (c t)").bitcast(F32)
+    return flat.rearrange("p (c u) -> p c u", u=2)
+
+
+def tile_cross_module_pb_kernel(tc, q2, k1, v2, wc1, bc1, gamma2, x2, out):
+    nc = tc.nc
+    with ExitStack() as ctx:
+        const = ctx.enter_context(tc.tile_pool(name="const", bufs=1))
+        keep = ctx.enter_context(tc.tile_pool(name="keep", bufs=1))
+        work = ctx.enter_context(tc.tile_pool(name="work", bufs=4))
+        result = ctx.enter_context(tc.tile_pool(name="result", bufs=6))
+        psum_q2 = ctx.enter_context(tc.psum_pool(name="psum_q2", bufs=1))
+        psum_agg = ctx.enter_context(tc.psum_pool(name="psum_agg", bufs=2))
+        psum_wide = ctx.enter_context(tc.psum_pool(name="psum_wide", bufs=4))
+
+        q2_row = const.tile([P, PIX], BF16)
+        nc.vector.memset(q2_row[:], 0.0)
+        nc.sync.dma_start(out=q2_row[0:1, :], in_=q2)
+        k1_bf = const.tile([P, K_PASSES * 2, 2], BF16)
+        nc.sync.dma_start(out=k1_bf[:], in_=k1.rearrange("b (a p e) -> p (b a) e", p=P, e=2))
+        gamma_bf = const.tile([P, 1], BF16)
+        nc.scalar.dma_start(out=gamma_bf[:], in_=gamma2.partition_broadcast(P))
+        bias_bf = const.tile([P, O_TILES], BF16)
+        nc.scalar.dma_start(out=bias_bf[:], in_=bc1.rearrange("(r j) -> r j", j=O_TILES))
+        v2_sb = keep.tile([P, C_TILES, PIX], BF16)
+        v2_rows = v2.rearrange("b (u r e) k -> (b u) r e k", r=P, e=2)
+        for u in range(2):
+            nc.sync.dma_start(out=v2_sb[:, 2 * u : 2 * u + 2, :], in_=v2_rows[u])
+        w_sb = keep.tile([P, O_TILES, C_IN], BF16)
+        w_rows = wc1.rearrange("(r j) c -> r j c", j=O_TILES)
+        for half in range(2):
+            j_half = slice(half * O_TILES // 2, (half + 1) * O_TILES // 2)
+            nc.sync.dma_start(out=w_sb[:, j_half, :], in_=w_rows[:, j_half, :])
+        x2_sb = keep.tile([P, O_TILES, PIX], BF16)
+        x2_rows = x2.rearrange("b (r j) h w -> r (b j) (h w)", j=O_TILES)
+        for pair in range(O_TILES // 2):
+            j_pair = slice(2 * pair, 2 * pair + 2)
+            nc.sync.dma_start(out=x2_sb[:, j_pair, :], in_=x2_rows[:, j_pair, :])
+        out_rows = out.rearrange("b (r j) h w -> r (b j) (h w)", j=O_TILES)
+
+        ones = const.tile([P, P], BF16)
+        nc.vector.memset(ones[:], 1.0)
+        ident = const.tile([P, P], F32)
+        make_identity(nc, ident[:])
+        k1_col = const.tile([P, K_PASSES * PACK], F32)
+        nc.vector.tensor_copy(out=k1_col[:], in_=k1_bf[:].rearrange("p a e -> p (a e)"))
+        gamma_col = const.tile([P, 1], F32)
+        nc.vector.tensor_copy(out=gamma_col[:], in_=gamma_bf[:])
+        gamma_bias = const.tile([P, O_TILES], F32)
+        nc.vector.tensor_scalar(
+            out=gamma_bias[:], in0=bias_bf[:], scalar1=gamma_col[:, 0:1], scalar2=None, op0=ALU.mult
+        )
+
+        q2_all = []
+        for h in range(PIX // BANK):
+            q2_bank = psum_q2.tile([P, BANK], F32, name="q2_bank%d" % h)
+            nc.tensor.matmul(
+                out=q2_bank[:], lhsT=ones[:], rhs=q2_row[:, h * BANK : (h + 1) * BANK], start=True, stop=True
+            )
+            q2_all.append(q2_bank)
+
+        def transpose_two_tiles(rows_sb, first_tile, word_base, grouped_cols, copy):
+            flipped = psum_wide.tile([P, 2, 2 * P], F32, tag="wide")
+            for u in range(2):
+                for i in range(2):
+                    words = rows_sb[:, first_tile + i, :].bitcast(F32)
+                    nc.tensor.transpose(
+                        flipped[:, u, i * P : (i + 1) * P],
+                        words[:, word_base + u * P : word_base + (u + 1) * P],
+                        ident[:],
+                    )
+            copy(out=word_view(grouped_cols), in_=flipped[:].rearrange("p u r -> p r u"))
+
+        v2_grouped = keep.tile([P, K_PASSES, C_IN, PACK], BF16, align_bytes=64)
+        v2_codes = keep.tile([P, K_PASSES, C_IN], U32, align_bytes=64)
+        v2_scales = keep.tile([P, K_PASSES, C_IN], U8, align_bytes=64)
+        for g in range(K_PASSES):
+            for t in range(0, C_TILES, 2):
+                transpose_two_tiles(
+                    v2_sb, t, g * 2 * P, v2_grouped[:, g, t * P : (t + 2) * P, :], nc.vector.tensor_copy
+                )
+        for g in range(K_PASSES):
+            nc.vector.quantize_mx(
+                out=v2_codes[:, g, :].bitcast(FP8X4),
+                scales=v2_scales[:, g, :],
+                in_=v2_grouped[:, g, :, :].rearrange("p c t -> p (c t)"),
+            )
+
+        w_grouped = keep.tile([P, C_OUT, PACK], BF16, align_bytes=64)
+        w_codes = keep.tile([P, C_OUT], U32, align_bytes=64)
+        w_scales = keep.tile([P, C_OUT], U8, align_bytes=64)
+        for j in range(0, O_TILES, 2):
+            transpose_two_tiles(w_sb, j, 0, w_grouped[:, j * P : (j + 2) * P, :], nc.scalar.copy)
+        for half in range(2):
+            o_half = slice(half * C_OUT // 2, (half + 1) * C_OUT // 2)
+            nc.vector.quantize_mx(
+                out=w_codes[:, o_half].bitcast(FP8X4),
+                scales=w_scales[:, o_half],
+                in_=w_grouped[:, o_half, :].rearrange("p o t -> p (o t)"),
+            )
+
+        x2_biased = keep.tile([P, O_TILES, PIX], F32)
+        for j in range(0, O_TILES, 2):
+            nc.vector.tensor_scalar(
+                out=x2_biased[:, j, :], in0=x2_sb[:, j, :], scalar1=gamma_bias[:, j : j + 1], scalar2=None, op0=ALU.add
+            )
+            nc.scalar.activation(
+                out=x2_biased[:, j + 1, :], in_=x2_sb[:, j + 1, :], func=ACT.Identity, bias=gamma_bias[:, j + 1 : j + 2]
+            )
+
+        for chunk in range(PIX // M_CHUNK):
+            m_lo = chunk * M_CHUNK
+            q2_cols = q2_all[m_lo // BANK][:, m_lo % BANK : m_lo % BANK + M_CHUNK]
+
+            gate = work.tile([P, K_PASSES * PACK, M_CHUNK], BF16)
+            for row in range(K_PASSES * PACK):
+                nc.scalar.activation(
+                    out=gate[:, row, :], in_=q2_cols, func=ACT.Sigmoid, scale=k1_col[:, row : row + 1]
+                )
+            gate_grouped = work.tile([P, K_PASSES, M_CHUNK, PACK], BF16, align_bytes=64)
+            for g in range(K_PASSES):
+                nc.vector.tensor_copy(
+                    out=gate_grouped[:, g, :, :].rearrange("p (c i) t -> p c t i", i=4),
+                    in_=gate[:, g * PACK : (g + 1) * PACK, :].rearrange("p t (c i) -> p c t i", i=4),
+                )
+            gate_codes = work.tile([P, K_PASSES, M_CHUNK], U32, align_bytes=64)
+            gate_scales = work.tile([P, K_PASSES, M_CHUNK], U8, align_bytes=64)
+            for g in range(K_PASSES):
+                nc.vector.quantize_mx(
+                    out=gate_codes[:, g, :].bitcast(FP8X4),
+                    scales=gate_scales[:, g, :],
+                    in_=gate_grouped[:, g, :, :].rearrange("p m t -> p (m t)"),
+                )
+
+            agg_grouped = work.tile([P, M_CHUNK, PACK], BF16, align_bytes=64)
+            for sub in range(M_CHUNK // M_SUB):
+                m_sub = slice(sub * M_SUB, (sub + 1) * M_SUB)
+                agg_bank = psum_agg.tile([P, C_TILES, M_SUB], F32)
+                for t in range(C_TILES):
+                    c_cols = slice(t * P, (t + 1) * P)
+                    for g in range(K_PASSES):
+                        nc.tensor.matmul_mx(
+                            out=agg_bank[:, t, :],
+                            lhsT=v2_codes[:, g, c_cols].bitcast(FP8X4),
+                            lhsT_scale=v2_scales[:, g, c_cols],
+                            rhs=gate_codes[:, g, m_sub].bitcast(FP8X4),
+                            rhs_scale=gate_scales[:, g, m_sub],
+                            start=(g == 0),
+                            stop=(g == K_PASSES - 1),
+                        )
+                nc.scalar.copy(out=agg_grouped[:, m_sub, :], in_=agg_bank[:].rearrange("p t m -> p m t"))
+            agg_codes = work.tile([P, M_CHUNK], U32, align_bytes=64)
+            agg_scales = work.tile([P, M_CHUNK], U8, align_bytes=64)
+            nc.vector.quantize_mx(
+                out=agg_codes[:].bitcast(FP8X4),
+                scales=agg_scales[:],
+                in_=agg_grouped[:].rearrange("p m t -> p (m t)"),
+            )
+
+            for j in range(0, O_TILES, 2):
+                y_bank = psum_wide.tile([P, 2, M_CHUNK], F32, tag="wide")
+                for i in range(2):
+                    o_cols = slice((j + i) * P, (j + i + 1) * P)
+                    nc.tensor.matmul_mx(
+                        out=y_bank[:, i, :],
+                        lhsT=w_codes[:, o_cols].bitcast(FP8X4),
+                        lhsT_scale=w_scales[:, o_cols],
+                        rhs=agg_codes[:].bitcast(FP8X4),
+                        rhs_scale=agg_scales[:],
+                        start=True,
+                        stop=True,
+                    )
+                out_sb = result.tile([P, 2, M_CHUNK], F32)
+                nc.vector.scalar_tensor_tensor(
+                    out=out_sb[:],
+                    in0=y_bank[:],
+                    scalar=gamma_col[:, 0:1],
+                    in1=x2_biased[:, j : j + 2, m_lo : m_lo + M_CHUNK],
+                    op0=ALU.mult,
+                    op1=ALU.add,
+                )
+                nc.sync.dma_start(out=out_rows[:, j : j + 2, m_lo : m_lo + M_CHUNK], in_=out_sb[:])

@@ -55,16 +55,15 @@ def tile_cross_module_pb_kernel(tc, q2, k1, v2, wc1, bc1, gamma2, x2, out):
         v2_rows = v2.rearrange("b (u r e) k -> (b u) r e k", r=P, e=2)
         for u in range(2):
             nc.sync.dma_start(out=v2_sb[:, 2 * u : 2 * u + 2, :], in_=v2_rows[u])
+        x2_sb = keep.tile([P, O_TILES, PIX], BF16)
+        x2_rows = x2.rearrange("b (r j) h w -> r (b j) (h w)", j=O_TILES)
+        nc.sync.dma_start(out=x2_sb[:, :, 0 : PIX // 2], in_=x2_rows[:, :, 0 : PIX // 2])
         w_sb = keep.tile([P, O_TILES, C_IN], BF16)
         w_rows = wc1.rearrange("(r j) c -> r j c", j=O_TILES)
         for half in range(2):
             j_half = slice(half * O_TILES // 2, (half + 1) * O_TILES // 2)
             nc.sync.dma_start(out=w_sb[:, j_half, :], in_=w_rows[:, j_half, :])
-        x2_sb = keep.tile([P, O_TILES, PIX], BF16)
-        x2_rows = x2.rearrange("b (r j) h w -> r (b j) (h w)", j=O_TILES)
-        for pair in range(O_TILES // 2):
-            j_pair = slice(2 * pair, 2 * pair + 2)
-            nc.sync.dma_start(out=x2_sb[:, j_pair, :], in_=x2_rows[:, j_pair, :])
+        nc.sync.dma_start(out=x2_sb[:, :, PIX // 2 : PIX], in_=x2_rows[:, :, PIX // 2 : PIX])
         out_rows = out.rearrange("b (r j) h w -> r (b j) (h w)", j=O_TILES)
 
         ones = const.tile([P, P], BF16)
@@ -129,13 +128,17 @@ def tile_cross_module_pb_kernel(tc, q2, k1, v2, wc1, bc1, gamma2, x2, out):
             )
 
         x2_biased = keep.tile([P, O_TILES, PIX], F32)
-        for j in range(0, O_TILES, 2):
-            nc.vector.tensor_scalar(
-                out=x2_biased[:, j, :], in0=x2_sb[:, j, :], scalar1=gamma_bias[:, j : j + 1], scalar2=None, op0=ALU.add
-            )
-            nc.scalar.activation(
-                out=x2_biased[:, j + 1, :], in_=x2_sb[:, j + 1, :], func=ACT.Identity, bias=gamma_bias[:, j + 1 : j + 2]
-            )
+        for half in range(2):
+            m_half = slice(half * PIX // 2, (half + 1) * PIX // 2)
+            for j in range(O_TILES):
+                nc.gpsimd.tensor_scalar(
+                    out=x2_biased[:, j, m_half],
+                    in0=x2_sb[:, j, m_half],
+                    scalar1=1.0,
+                    scalar2=gamma_bias[:, j : j + 1],
+                    op0=ALU.mult,
+                    op1=ALU.add,
+                )
 
         for chunk in range(PIX // M_CHUNK):
             m_lo = chunk * M_CHUNK

@@ -43,12 +43,16 @@ def tile_cross_module_pb_kernel(tc, q2, k1, v2, wc1, bc1, gamma2, x2, out):
         psum_wide = ctx.enter_context(tc.psum_pool(name="psum_wide", bufs=4))
 
         q2_row = const.tile([P, PIX], BF16)
-        nc.vector.memset(q2_row[:], 0.0)
+        nc.vector.memset(q2_row[:].bitcast(U32), 0)
         nc.sync.dma_start(out=q2_row[0:1, :], in_=q2)
         k1_bf = const.tile([P, K_PASSES * 2, 2], BF16)
         nc.sync.dma_start(out=k1_bf[:], in_=k1.rearrange("b (a p e) -> p (b a) e", p=P, e=2))
         gamma_bf = const.tile([P, 1], BF16)
         nc.scalar.dma_start(out=gamma_bf[:], in_=gamma2.partition_broadcast(P))
+        table_probe = const.tile([P, 1], F32)
+        nc.vector.memset(table_probe[:], 0.0)
+        table_out = const.tile([P, 1], F32)
+        nc.scalar.activation(out=table_out[:], in_=table_probe[:], func=ACT.Sigmoid)
         bias_bf = const.tile([P, O_TILES], BF16)
         nc.scalar.dma_start(out=bias_bf[:], in_=bc1.rearrange("(r j) -> r j", j=O_TILES))
         v2_sb = keep.tile([P, C_TILES, PIX], BF16)

@@ -38,37 +38,44 @@ def tile_cross_module_pb_kernel(tc, q2, k1, v2, wc1, bc1, gamma2, x2, out):
         keep = ctx.enter_context(tc.tile_pool(name="keep", bufs=1))
         work = ctx.enter_context(tc.tile_pool(name="work", bufs=4))
         result = ctx.enter_context(tc.tile_pool(name="result", bufs=6))
-        psum_q2 = ctx.enter_context(tc.psum_pool(name="psum_q2", bufs=1))
+        psum_z = ctx.enter_context(tc.psum_pool(name="psum_z", bufs=2))
         psum_agg = ctx.enter_context(tc.psum_pool(name="psum_agg", bufs=2))
         psum_wide = ctx.enter_context(tc.psum_pool(name="psum_wide", bufs=4))
+        ctx.enter_context(tc.manual_schedule())
 
         q2_row = const.tile([P, PIX], BF16)
         nc.vector.memset(q2_row[:].bitcast(U32), 0)
-        nc.sync.dma_start(out=q2_row[0:1, :], in_=q2)
+        k1_row = const.tile([P, PIX], BF16)
+        nc.gpsimd.memset(k1_row[:].bitcast(U32), 0)
         k1_bf = const.tile([P, K_PASSES * 2, 2], BF16)
         nc.sync.dma_start(out=k1_bf[:], in_=k1.rearrange("b (a p e) -> p (b a) e", p=P, e=2))
-        gamma_bf = const.tile([P, 1], BF16)
-        nc.scalar.dma_start(out=gamma_bf[:], in_=gamma2.partition_broadcast(P))
-        table_probe = const.tile([P, 1], F32)
-        nc.vector.memset(table_probe[:], 0.0)
-        table_out = const.tile([P, 1], F32)
-        nc.scalar.activation(out=table_out[:], in_=table_probe[:], func=ACT.Sigmoid)
-        bias_bf = const.tile([P, O_TILES], BF16)
-        nc.scalar.dma_start(out=bias_bf[:], in_=bc1.rearrange("(r j) -> r j", j=O_TILES))
+        nc.sync.dma_start(out=k1_row[0:1, :], in_=k1)
+        nc.sync.dma_start(out=q2_row[0:1, :], in_=q2)
         v2_sb = keep.tile([P, C_TILES, PIX], BF16)
         v2_rows = v2.rearrange("b (u r e) k -> (b u) r e k", r=P, e=2)
         for u in range(2):
             nc.sync.dma_start(out=v2_sb[:, 2 * u : 2 * u + 2, :], in_=v2_rows[u])
         x2_sb = keep.tile([P, O_TILES, PIX], BF16)
         x2_rows = x2.rearrange("b (r j) h w -> r (b j) (h w)", j=O_TILES)
-        nc.sync.dma_start(out=x2_sb[:, :, 0 : PIX // 2], in_=x2_rows[:, :, 0 : PIX // 2])
+        x2_parts = (slice(0, M_CHUNK), slice(M_CHUNK, PIX // 2), slice(PIX // 2, PIX))
+        nc.sync.dma_start(out=x2_sb[:, :, x2_parts[0]], in_=x2_rows[:, :, x2_parts[0]])
         w_sb = keep.tile([P, O_TILES, C_IN], BF16)
         w_rows = wc1.rearrange("(r j) c -> r j c", j=O_TILES)
         for half in range(2):
             j_half = slice(half * O_TILES // 2, (half + 1) * O_TILES // 2)
             nc.sync.dma_start(out=w_sb[:, j_half, :], in_=w_rows[:, j_half, :])
-        nc.sync.dma_start(out=x2_sb[:, :, PIX // 2 : PIX], in_=x2_rows[:, :, PIX // 2 : PIX])
+        for part in x2_parts[1:]:
+            nc.sync.dma_start(out=x2_sb[:, :, part], in_=x2_rows[:, :, part])
         out_rows = out.rearrange("b (r j) h w -> r (b j) (h w)", j=O_TILES)
+        gamma_bf = const.tile([P, 1], BF16)
+        nc.scalar.dma_start(out=gamma_bf[:], in_=gamma2.partition_broadcast(P))
+        bias_bf = const.tile([P, O_TILES], BF16)
+        nc.scalar.dma_start(out=bias_bf[:], in_=bc1.rearrange("(r j) -> r j", j=O_TILES))
+
+        table_probe = const.tile([P, 1], F32)
+        nc.vector.memset(table_probe[:], 0.0)
+        table_out = const.tile([P, 1], F32)
+        nc.scalar.activation(out=table_out[:], in_=table_probe[:], func=ACT.Sigmoid)
 
         ones = const.tile([P, P], BF16)
         nc.vector.memset(ones[:], 1.0)
@@ -82,48 +89,130 @@ def tile_cross_module_pb_kernel(tc, q2, k1, v2, wc1, bc1, gamma2, x2, out):
         nc.vector.tensor_scalar(
             out=gamma_bias[:], in0=bias_bf[:], scalar1=gamma_col[:, 0:1], scalar2=None, op0=ALU.mult
         )
+        k1_stat = const.tile([P, K_PASSES * PACK, P], BF16)
+        nc.gpsimd.tensor_scalar(
+            out=k1_stat[:].rearrange("q (a e) p -> q a e p", e=2),
+            in0=k1_row[:].rearrange("q (a p e) -> q a e p", p=P, e=2),
+            scalar1=1.0,
+            scalar2=0.0,
+            op0=ALU.mult,
+            op1=ALU.add,
+        )
 
-        q2_all = []
-        for h in range(PIX // BANK):
-            q2_bank = psum_q2.tile([P, BANK], F32, name="q2_bank%d" % h)
-            nc.tensor.matmul(
-                out=q2_bank[:], lhsT=ones[:], rhs=q2_row[:, h * BANK : (h + 1) * BANK], start=True, stop=True
+        x2_biased = keep.tile([P, O_TILES, PIX], F32)
+        for part in x2_parts:
+            for j in range(O_TILES):
+                nc.gpsimd.tensor_scalar(
+                    out=x2_biased[:, j, part],
+                    in0=x2_sb[:, j, part],
+                    scalar1=1.0,
+                    scalar2=gamma_bias[:, j : j + 1],
+                    op0=ALU.mult,
+                    op1=ALU.add,
+                )
+
+        pairs = PIX // M_CHUNK
+        subs = M_CHUNK // M_SUB
+        gate_grouped = [work.tile([P, K_PASSES, M_CHUNK, PACK], BF16, name="gate_grouped", align_bytes=64) for p in range(pairs)]
+        gate_codes = [work.tile([P, K_PASSES, M_CHUNK], U32, name="gate_codes", align_bytes=64) for p in range(pairs)]
+        gate_scales = [work.tile([P, K_PASSES, M_CHUNK], U8, name="gate_scales", align_bytes=64) for p in range(pairs)]
+        agg_grouped = [work.tile([P, M_CHUNK, PACK], BF16, name="agg_grouped", align_bytes=64) for p in range(pairs)]
+        agg_codes = [work.tile([P, M_CHUNK], U32, name="agg_codes", align_bytes=64) for p in range(pairs)]
+        agg_scales = [work.tile([P, M_CHUNK], U8, name="agg_scales", align_bytes=64) for p in range(pairs)]
+
+        gate_rows = keep.tile([P, K_PASSES * PACK, M_CHUNK], BF16)
+
+        def gate_first_sigmoid():
+            q2_cols = psum_agg.tile([P, M_CHUNK], F32, tag="agg")
+            nc.tensor.matmul(out=q2_cols[:], lhsT=ones[:], rhs=q2_row[:, 0:M_CHUNK], start=True, stop=True)
+            for row in range(K_PASSES * PACK):
+                nc.scalar.activation(
+                    out=gate_rows[:, row, :], in_=q2_cols[:], func=ACT.Sigmoid, scale=k1_col[:, row : row + 1]
+                )
+
+        def gate_first_interleave(g):
+            nc.vector.tensor_copy(
+                out=gate_grouped[0][:, g, :, :].rearrange("p (c i) t -> p c t i", i=4),
+                in_=gate_rows[:, g * PACK : (g + 1) * PACK, :].rearrange("p t (c i) -> p c t i", i=4),
             )
-            q2_all.append(q2_bank)
 
-        def transpose_two_tiles(rows_sb, first_tile, word_base, grouped_cols, copy):
+        logits = {}
+
+        def gate_logits(unit, g):
+            z_bank = psum_z.tile([P, PACK, M_SUB], F32, tag="z")
+            for t in range(PACK):
+                nc.tensor.matmul(
+                    out=z_bank[:, t, :],
+                    lhsT=k1_stat[:, g * PACK + t, :],
+                    rhs=q2_row[:, unit * M_SUB : (unit + 1) * M_SUB],
+                    start=True,
+                    stop=True,
+                )
+            logits[unit, g] = z_bank
+
+        def gate_sigmoid(unit, g):
+            pair, sub = divmod(unit, subs)
+            nc.scalar.activation(
+                out=gate_grouped[pair][:, g, sub * M_SUB : (sub + 1) * M_SUB, :],
+                in_=logits[unit, g][:].rearrange("p t m -> p m t"),
+                func=ACT.Sigmoid,
+            )
+
+        def gate_quantise(pair):
+            for g in range(K_PASSES):
+                nc.vector.quantize_mx(
+                    out=gate_codes[pair][:, g, :].bitcast(FP8X4),
+                    scales=gate_scales[pair][:, g, :],
+                    in_=gate_grouped[pair][:, g, :, :].rearrange("p m t -> p (m t)"),
+                )
+
+        def transpose_two_tiles(rows_sb, first_tile, word_base):
             flipped = psum_wide.tile([P, 2, 2 * P], F32, tag="wide")
-            for u in range(2):
-                for i in range(2):
+            for i in range(2):
+                for u in range(2):
                     words = rows_sb[:, first_tile + i, :].bitcast(F32)
                     nc.tensor.transpose(
                         flipped[:, u, i * P : (i + 1) * P],
                         words[:, word_base + u * P : word_base + (u + 1) * P],
                         ident[:],
                     )
+            return flipped
+
+        def lay_words(copy, flipped, grouped_cols):
             copy(out=word_view(grouped_cols), in_=flipped[:].rearrange("p u r -> p r u"))
 
         v2_grouped = keep.tile([P, K_PASSES, C_IN, PACK], BF16, align_bytes=64)
         v2_codes = keep.tile([P, K_PASSES, C_IN], U32, align_bytes=64)
         v2_scales = keep.tile([P, K_PASSES, C_IN], U8, align_bytes=64)
-        for g in range(K_PASSES):
-            for t in range(0, C_TILES, 2):
-                transpose_two_tiles(
-                    v2_sb, t, g * 2 * P, v2_grouped[:, g, t * P : (t + 2) * P, :], nc.vector.tensor_copy
-                )
-        for g in range(K_PASSES):
-            nc.vector.quantize_mx(
-                out=v2_codes[:, g, :].bitcast(FP8X4),
-                scales=v2_scales[:, g, :],
-                in_=v2_grouped[:, g, :, :].rearrange("p c t -> p (c t)"),
-            )
-
         w_grouped = keep.tile([P, C_OUT, PACK], BF16, align_bytes=64)
         w_codes = keep.tile([P, C_OUT], U32, align_bytes=64)
         w_scales = keep.tile([P, C_OUT], U8, align_bytes=64)
-        for j in range(0, O_TILES, 2):
-            transpose_two_tiles(w_sb, j, 0, w_grouped[:, j * P : (j + 2) * P, :], nc.scalar.copy)
-        for half in range(2):
+
+        flipped_v2 = {}
+
+        def v2_transposes(t, g):
+            flipped_v2[t, g] = transpose_two_tiles(v2_sb, t, g * 2 * P)
+
+        def v2_copy(copy, t, g):
+            lay_words(copy, flipped_v2[t, g], v2_grouped[:, g, t * P : (t + 2) * P, :])
+
+        flipped_w = {}
+
+        def w_transposes(j):
+            flipped_w[j] = transpose_two_tiles(w_sb, j, 0)
+
+        def w_copy(copy, j):
+            lay_words(copy, flipped_w[j], w_grouped[:, j * P : (j + 2) * P, :])
+
+        def v2_quantise():
+            for g in range(K_PASSES):
+                nc.vector.quantize_mx(
+                    out=v2_codes[:, g, :].bitcast(FP8X4),
+                    scales=v2_scales[:, g, :],
+                    in_=v2_grouped[:, g, :, :].rearrange("p c t -> p (c t)"),
+                )
+
+        def w_quantise(half):
             o_half = slice(half * C_OUT // 2, (half + 1) * C_OUT // 2)
             nc.vector.quantize_mx(
                 out=w_codes[:, o_half].bitcast(FP8X4),
@@ -131,88 +220,130 @@ def tile_cross_module_pb_kernel(tc, q2, k1, v2, wc1, bc1, gamma2, x2, out):
                 in_=w_grouped[:, o_half, :].rearrange("p o t -> p (o t)"),
             )
 
-        x2_biased = keep.tile([P, O_TILES, PIX], F32)
-        for half in range(2):
-            m_half = slice(half * PIX // 2, (half + 1) * PIX // 2)
-            for j in range(O_TILES):
-                nc.gpsimd.tensor_scalar(
-                    out=x2_biased[:, j, m_half],
-                    in0=x2_sb[:, j, m_half],
-                    scalar1=1.0,
-                    scalar2=gamma_bias[:, j : j + 1],
-                    op0=ALU.mult,
-                    op1=ALU.add,
-                )
+        agg_banks = {}
 
-        for chunk in range(PIX // M_CHUNK):
-            m_lo = chunk * M_CHUNK
-            q2_cols = q2_all[m_lo // BANK][:, m_lo % BANK : m_lo % BANK + M_CHUNK]
+        def agg_matmul(unit):
+            pair, sub = divmod(unit, subs)
+            m_sub = slice(sub * M_SUB, (sub + 1) * M_SUB)
+            agg_bank = psum_agg.tile([P, C_TILES, M_SUB], F32, tag="agg")
+            for t in range(C_TILES):
+                c_cols = slice(t * P, (t + 1) * P)
+                for g in range(K_PASSES):
+                    nc.tensor.matmul_mx(
+                        out=agg_bank[:, t, :],
+                        lhsT=v2_codes[:, g, c_cols].bitcast(FP8X4),
+                        lhsT_scale=v2_scales[:, g, c_cols],
+                        rhs=gate_codes[pair][:, g, m_sub].bitcast(FP8X4),
+                        rhs_scale=gate_scales[pair][:, g, m_sub],
+                        start=(g == 0),
+                        stop=(g == K_PASSES - 1),
+                    )
+            agg_banks[unit] = agg_bank
 
-            gate = work.tile([P, K_PASSES * PACK, M_CHUNK], BF16)
-            for row in range(K_PASSES * PACK):
-                nc.scalar.activation(
-                    out=gate[:, row, :], in_=q2_cols, func=ACT.Sigmoid, scale=k1_col[:, row : row + 1]
-                )
-            gate_grouped = work.tile([P, K_PASSES, M_CHUNK, PACK], BF16, align_bytes=64)
-            for g in range(K_PASSES):
-                nc.vector.tensor_copy(
-                    out=gate_grouped[:, g, :, :].rearrange("p (c i) t -> p c t i", i=4),
-                    in_=gate[:, g * PACK : (g + 1) * PACK, :].rearrange("p t (c i) -> p c t i", i=4),
-                )
-            gate_codes = work.tile([P, K_PASSES, M_CHUNK], U32, align_bytes=64)
-            gate_scales = work.tile([P, K_PASSES, M_CHUNK], U8, align_bytes=64)
-            for g in range(K_PASSES):
-                nc.vector.quantize_mx(
-                    out=gate_codes[:, g, :].bitcast(FP8X4),
-                    scales=gate_scales[:, g, :],
-                    in_=gate_grouped[:, g, :, :].rearrange("p m t -> p (m t)"),
-                )
-
-            agg_grouped = work.tile([P, M_CHUNK, PACK], BF16, align_bytes=64)
-            for sub in range(M_CHUNK // M_SUB):
-                m_sub = slice(sub * M_SUB, (sub + 1) * M_SUB)
-                agg_bank = psum_agg.tile([P, C_TILES, M_SUB], F32)
-                for t in range(C_TILES):
-                    c_cols = slice(t * P, (t + 1) * P)
-                    for g in range(K_PASSES):
-                        nc.tensor.matmul_mx(
-                            out=agg_bank[:, t, :],
-                            lhsT=v2_codes[:, g, c_cols].bitcast(FP8X4),
-                            lhsT_scale=v2_scales[:, g, c_cols],
-                            rhs=gate_codes[:, g, m_sub].bitcast(FP8X4),
-                            rhs_scale=gate_scales[:, g, m_sub],
-                            start=(g == 0),
-                            stop=(g == K_PASSES - 1),
-                        )
-                nc.scalar.copy(out=agg_grouped[:, m_sub, :], in_=agg_bank[:].rearrange("p t m -> p m t"))
-            agg_codes = work.tile([P, M_CHUNK], U32, align_bytes=64)
-            agg_scales = work.tile([P, M_CHUNK], U8, align_bytes=64)
-            nc.vector.quantize_mx(
-                out=agg_codes[:].bitcast(FP8X4),
-                scales=agg_scales[:],
-                in_=agg_grouped[:].rearrange("p m t -> p (m t)"),
+        def agg_copy(unit):
+            pair, sub = divmod(unit, subs)
+            nc.scalar.copy(
+                out=agg_grouped[pair][:, sub * M_SUB : (sub + 1) * M_SUB, :],
+                in_=agg_banks[unit][:].rearrange("p t m -> p m t"),
             )
 
-            for j in range(0, O_TILES, 2):
-                y_bank = psum_wide.tile([P, 2, M_CHUNK], F32, tag="wide")
-                for i in range(2):
-                    o_cols = slice((j + i) * P, (j + i + 1) * P)
-                    nc.tensor.matmul_mx(
-                        out=y_bank[:, i, :],
-                        lhsT=w_codes[:, o_cols].bitcast(FP8X4),
-                        lhsT_scale=w_scales[:, o_cols],
-                        rhs=agg_codes[:].bitcast(FP8X4),
-                        rhs_scale=agg_scales[:],
-                        start=True,
-                        stop=True,
-                    )
-                out_sb = result.tile([P, 2, M_CHUNK], F32)
-                nc.vector.scalar_tensor_tensor(
-                    out=out_sb[:],
-                    in0=y_bank[:],
-                    scalar=gamma_col[:, 0:1],
-                    in1=x2_biased[:, j : j + 2, m_lo : m_lo + M_CHUNK],
-                    op0=ALU.mult,
-                    op1=ALU.add,
+        def agg_quantise(pair):
+            nc.vector.quantize_mx(
+                out=agg_codes[pair][:].bitcast(FP8X4),
+                scales=agg_scales[pair][:],
+                in_=agg_grouped[pair][:].rearrange("p m t -> p (m t)"),
+            )
+
+        y_psum = {}
+
+        def y_matmul(pair, j):
+            y_bank = psum_wide.tile([P, 2, M_CHUNK], F32, tag="wide")
+            for i in range(2):
+                o_cols = slice((j + i) * P, (j + i + 1) * P)
+                nc.tensor.matmul_mx(
+                    out=y_bank[:, i, :],
+                    lhsT=w_codes[:, o_cols].bitcast(FP8X4),
+                    lhsT_scale=w_scales[:, o_cols],
+                    rhs=agg_codes[pair][:].bitcast(FP8X4),
+                    rhs_scale=agg_scales[pair][:],
+                    start=True,
+                    stop=True,
                 )
-                nc.sync.dma_start(out=out_rows[:, j : j + 2, m_lo : m_lo + M_CHUNK], in_=out_sb[:])
+            y_psum[pair, j] = y_bank
+
+        def y_finish(pair, j):
+            m_cols = slice(pair * M_CHUNK, (pair + 1) * M_CHUNK)
+            out_sb = result.tile([P, 2, M_CHUNK], F32, name="out_sb")
+            nc.vector.scalar_tensor_tensor(
+                out=out_sb[:],
+                in0=y_psum[pair, j][:],
+                scalar=gamma_col[:, 0:1],
+                in1=x2_biased[:, j : j + 2, m_cols],
+                op0=ALU.mult,
+                op1=ALU.add,
+            )
+            nc.sync.dma_start(out=out_rows[:, j : j + 2, m_cols], in_=out_sb[:])
+
+        dve_copy, act_copy = nc.vector.tensor_copy, nc.scalar.copy
+
+        def gate(unit, g):
+            gate_logits(unit, g)
+            gate_sigmoid(unit, g)
+
+        gate_first_sigmoid()
+        gate(2, 0)
+        gate(2, 1)
+        for t in (0, 2):
+            for g in range(K_PASSES):
+                v2_transposes(t, g)
+        gate_first_interleave(0)
+        v2_copy(dve_copy, 0, 0)
+        v2_copy(dve_copy, 0, 1)
+        gate_first_interleave(1)
+        v2_copy(dve_copy, 2, 0)
+        v2_copy(dve_copy, 2, 1)
+        gate(3, 0)
+        gate(3, 1)
+        gate(4, 0)
+        gate(4, 1)
+        gate_quantise(0)
+        v2_quantise()
+        for j in range(0, O_TILES, 2):
+            w_transposes(j)
+        agg_matmul(0)
+        agg_matmul(1)
+        w_copy(act_copy, 0)
+        w_copy(act_copy, 2)
+        agg_copy(0)
+        agg_copy(1)
+        w_copy(act_copy, 4)
+        w_copy(act_copy, 6)
+        gate_quantise(1)
+        w_quantise(0)
+        agg_quantise(0)
+        w_quantise(1)
+        for pair in range(pairs):
+            for j in (0, 2):
+                y_matmul(pair, j)
+            if pair + 1 < pairs:
+                agg_matmul(2 * pair + 2)
+                agg_copy(2 * pair + 2)
+            for j in (4, 6):
+                y_matmul(pair, j)
+            if pair + 1 < pairs:
+                agg_matmul(2 * pair + 3)
+                agg_copy(2 * pair + 3)
+            if pair == 0:
+                for unit in (5, 6):
+                    for g in range(K_PASSES):
+                        gate(unit, g)
+            if pair == 1:
+                for g in range(K_PASSES):
+                    gate(7, g)
+            for j in (0, 2, 4):
+                y_finish(pair, j)
+            if pair + 1 < pairs:
+                agg_quantise(pair + 1)
+            y_finish(pair, 6)
+            if pair + 2 < pairs:
+                gate_quantise(pair + 2)

@@ -43,14 +43,15 @@ def tile_cross_module_pb_kernel(tc, q2, k1, v2, wc1, bc1, gamma2, x2, out):
         psum_wide = ctx.enter_context(tc.psum_pool(name="psum_wide", bufs=4))
         ctx.enter_context(tc.manual_schedule())
 
-        q2_row = const.tile([P, PIX], BF16)
+        q2_row = const.tile([P, PIX + 2], BF16)
         nc.vector.memset(q2_row[:].bitcast(U32), 0)
         k1_row = const.tile([P, PIX], BF16)
         nc.gpsimd.memset(k1_row[:].bitcast(U32), 0)
         k1_bf = const.tile([P, K_PASSES * 2, 2], BF16)
         nc.sync.dma_start(out=k1_bf[:], in_=k1.rearrange("b (a p e) -> p (b a) e", p=P, e=2))
         nc.sync.dma_start(out=k1_row[0:1, :], in_=k1)
-        nc.sync.dma_start(out=q2_row[0:1, :], in_=q2)
+        nc.sync.dma_start(out=q2_row[0:1, 0:PIX], in_=q2)
+        nc.sync.dma_start(out=q2_row[0:1, PIX : PIX + 1], in_=gamma2.rearrange("(a b) -> a b", a=1))
         v2_sb = keep.tile([P, C_TILES, PIX], BF16)
         v2_rows = v2.rearrange("b (u r e) k -> (b u) r e k", r=P, e=2)
         for u in range(2):
@@ -67,8 +68,6 @@ def tile_cross_module_pb_kernel(tc, q2, k1, v2, wc1, bc1, gamma2, x2, out):
         for part in x2_parts[1:]:
             nc.sync.dma_start(out=x2_sb[:, :, part], in_=x2_rows[:, :, part])
         out_rows = out.rearrange("b (r j) h w -> r (b j) (h w)", j=O_TILES)
-        gamma_bf = const.tile([P, 1], BF16)
-        nc.scalar.dma_start(out=gamma_bf[:], in_=gamma2.partition_broadcast(P))
         bias_bf = const.tile([P, O_TILES], BF16)
         nc.scalar.dma_start(out=bias_bf[:], in_=bc1.rearrange("(r j) -> r j", j=O_TILES))
 
@@ -84,7 +83,12 @@ def tile_cross_module_pb_kernel(tc, q2, k1, v2, wc1, bc1, gamma2, x2, out):
         k1_col = const.tile([P, K_PASSES * PACK], F32)
         nc.vector.tensor_copy(out=k1_col[:], in_=k1_bf[:].rearrange("p a e -> p (a e)"))
         gamma_col = const.tile([P, 1], F32)
-        nc.vector.tensor_copy(out=gamma_col[:], in_=gamma_bf[:])
+        q2_cols = psum_agg.tile([P, M_CHUNK + 1], F32, tag="agg")
+        nc.tensor.matmul(out=q2_cols[:, 0:M_CHUNK], lhsT=ones[:], rhs=q2_row[:, 0:M_CHUNK], start=True, stop=True)
+        nc.tensor.matmul(
+            out=q2_cols[:, M_CHUNK : M_CHUNK + 1], lhsT=ones[:], rhs=q2_row[:, PIX : PIX + 1], start=True, stop=True
+        )
+        nc.vector.tensor_copy(out=gamma_col[:], in_=q2_cols[:, M_CHUNK : M_CHUNK + 1])
         gamma_bias = const.tile([P, O_TILES], F32)
         nc.vector.tensor_scalar(
             out=gamma_bias[:], in0=bias_bf[:], scalar1=gamma_col[:, 0:1], scalar2=None, op0=ALU.mult
@@ -123,11 +127,9 @@ def tile_cross_module_pb_kernel(tc, q2, k1, v2, wc1, bc1, gamma2, x2, out):
         gate_rows = keep.tile([P, K_PASSES * PACK, M_CHUNK], BF16)
 
         def gate_first_sigmoid():
-            q2_cols = psum_agg.tile([P, M_CHUNK], F32, tag="agg")
-            nc.tensor.matmul(out=q2_cols[:], lhsT=ones[:], rhs=q2_row[:, 0:M_CHUNK], start=True, stop=True)
             for row in range(K_PASSES * PACK):
                 nc.scalar.activation(
-                    out=gate_rows[:, row, :], in_=q2_cols[:], func=ACT.Sigmoid, scale=k1_col[:, row : row + 1]
+                    out=gate_rows[:, row, :], in_=q2_cols[:, 0:M_CHUNK], func=ACT.Sigmoid, scale=k1_col[:, row : row + 1]
                 )
 
         def gate_first_interleave(g):

@@ -56,17 +56,16 @@ def tile_cross_module_pb_kernel(tc, q2, k1, v2, wc1, bc1, gamma2, x2, out):
         v2_rows = v2.rearrange("b (u r e) k -> (b u) r e k", r=P, e=2)
         for u in range(2):
             nc.sync.dma_start(out=v2_sb[:, 2 * u : 2 * u + 2, :], in_=v2_rows[u])
-        x2_sb = keep.tile([P, O_TILES, PIX], BF16)
-        x2_rows = x2.rearrange("b (r j) h w -> r (b j) (h w)", j=O_TILES)
-        x2_parts = (slice(0, M_CHUNK), slice(M_CHUNK, PIX // 2), slice(PIX // 2, PIX))
-        nc.sync.dma_start(out=x2_sb[:, :, x2_parts[0]], in_=x2_rows[:, :, x2_parts[0]])
         w_sb = keep.tile([P, O_TILES, C_IN], BF16)
         w_rows = wc1.rearrange("(r j) c -> r j c", j=O_TILES)
         for half in range(2):
             j_half = slice(half * O_TILES // 2, (half + 1) * O_TILES // 2)
             nc.sync.dma_start(out=w_sb[:, j_half, :], in_=w_rows[:, j_half, :])
-        for part in x2_parts[1:]:
-            nc.sync.dma_start(out=x2_sb[:, :, part], in_=x2_rows[:, :, part])
+        x2_sb = keep.tile([P, O_TILES, PIX], BF16)
+        x2_rows = x2.rearrange("b (r j) h w -> r (b j) (h w)", j=O_TILES)
+        for half in range(2):
+            m_half = slice(half * PIX // 2, (half + 1) * PIX // 2)
+            nc.sync.dma_start(out=x2_sb[:, :, m_half], in_=x2_rows[:, :, m_half])
         out_rows = out.rearrange("b (r j) h w -> r (b j) (h w)", j=O_TILES)
         bias_bf = const.tile([P, O_TILES], BF16)
         nc.scalar.dma_start(out=bias_bf[:], in_=bc1.rearrange("(r j) -> r j", j=O_TILES))
@@ -104,16 +103,23 @@ def tile_cross_module_pb_kernel(tc, q2, k1, v2, wc1, bc1, gamma2, x2, out):
         )
 
         x2_biased = keep.tile([P, O_TILES, PIX], F32)
-        for part in x2_parts:
-            for j in range(O_TILES):
-                nc.gpsimd.tensor_scalar(
-                    out=x2_biased[:, j, part],
-                    in0=x2_sb[:, j, part],
-                    scalar1=1.0,
-                    scalar2=gamma_bias[:, j : j + 1],
-                    op0=ALU.mult,
-                    op1=ALU.add,
-                )
+
+        def bias_on_vector(j, m_cols):
+            nc.vector.tensor_scalar(
+                out=x2_biased[:, j, m_cols],
+                in0=x2_sb[:, j, m_cols],
+                scalar1=gamma_bias[:, j : j + 1],
+                scalar2=None,
+                op0=ALU.add,
+            )
+
+        def bias_on_scalar(j, m_cols):
+            nc.scalar.activation(
+                out=x2_biased[:, j, m_cols],
+                in_=x2_sb[:, j, m_cols],
+                func=ACT.Identity,
+                bias=gamma_bias[:, j : j + 1],
+            )
 
         pairs = PIX // M_CHUNK
         subs = M_CHUNK // M_SUB
@@ -300,10 +306,10 @@ def tile_cross_module_pb_kernel(tc, q2, k1, v2, wc1, bc1, gamma2, x2, out):
                 v2_transposes(t, g)
         gate_first_interleave(0)
         v2_copy(dve_copy, 0, 0)
+        v2_copy(act_copy, 2, 0)
         v2_copy(dve_copy, 0, 1)
+        v2_copy(act_copy, 2, 1)
         gate_first_interleave(1)
-        v2_copy(dve_copy, 2, 0)
-        v2_copy(dve_copy, 2, 1)
         gate(3, 0)
         gate(3, 1)
         gate(4, 0)
@@ -312,40 +318,47 @@ def tile_cross_module_pb_kernel(tc, q2, k1, v2, wc1, bc1, gamma2, x2, out):
         v2_quantise()
         for j in range(0, O_TILES, 2):
             w_transposes(j)
-        agg_matmul(0)
-        agg_matmul(1)
-        w_copy(act_copy, 0)
-        w_copy(act_copy, 2)
-        agg_copy(0)
-        agg_copy(1)
         w_copy(act_copy, 4)
+        gate(5, 0)
+        agg_matmul(0)
+        agg_copy(0)
+        agg_matmul(1)
+        agg_copy(1)
         w_copy(act_copy, 6)
+        gate(5, 1)
+        w_copy(dve_copy, 0)
+        w_copy(dve_copy, 2)
         gate_quantise(1)
         w_quantise(0)
+        for j in range(0, O_TILES, 2):
+            bias_on_vector(j, slice(0, M_CHUNK))
+            bias_on_vector(j + 1, slice(0, M_CHUNK))
         agg_quantise(0)
         w_quantise(1)
+        gate_quantise(2)
         for pair in range(pairs):
-            for j in (0, 2):
-                y_matmul(pair, j)
             if pair + 1 < pairs:
                 agg_matmul(2 * pair + 2)
                 agg_copy(2 * pair + 2)
-            for j in (4, 6):
-                y_matmul(pair, j)
-            if pair + 1 < pairs:
                 agg_matmul(2 * pair + 3)
                 agg_copy(2 * pair + 3)
+            for j in (0, 2, 4, 6):
+                y_matmul(pair, j)
             if pair == 0:
-                for unit in (5, 6):
+                for unit in (6, 7):
                     for g in range(K_PASSES):
                         gate(unit, g)
             if pair == 1:
-                for g in range(K_PASSES):
-                    gate(7, g)
-            for j in (0, 2, 4):
-                y_finish(pair, j)
+                for j in (0, 1, 2, 3, 4, 5, 6, 7):
+                    bias_on_scalar(j, slice(3 * M_CHUNK, PIX))
+            y_finish(pair, 0)
+            y_finish(pair, 2)
             if pair + 1 < pairs:
                 agg_quantise(pair + 1)
+            y_finish(pair, 4)
             y_finish(pair, 6)
-            if pair + 2 < pairs:
-                gate_quantise(pair + 2)
+            if pair == 0:
+                gate_quantise(3)
+            if pair < 2:
+                for j in range(O_TILES):
+                    bias_on_vector(j, slice((pair + 1) * M_CHUNK, (pair + 2) * M_CHUNK))

@@ -75,6 +75,25 @@ def tile_cross_module_pb_kernel(tc, q2, k1, v2, wc1, bc1, gamma2, x2, out):
         table_out = const.tile([P, 1], F32)
         nc.scalar.activation(out=table_out[:], in_=table_probe[:], func=ACT.Sigmoid)
 
+        idle_grouped = const.tile([P, PACK * P], BF16, align_bytes=64)
+        nc.vector.memset(idle_grouped[:].bitcast(U32), 0)
+        idle_codes = const.tile([P, P], U32, align_bytes=64)
+        idle_scales = const.tile([P, P], U8, align_bytes=64)
+        nc.vector.quantize_mx(out=idle_codes[:].bitcast(FP8X4), scales=idle_scales[:], in_=idle_grouped[:])
+        idle_bank = psum_agg.tile([P, P], F32, tag="agg")
+
+        def idle_passes(count):
+            for repeat in range(count):
+                nc.tensor.matmul_mx(
+                    out=idle_bank[:],
+                    lhsT=idle_codes[:].bitcast(FP8X4),
+                    lhsT_scale=idle_scales[:],
+                    rhs=idle_codes[:].bitcast(FP8X4),
+                    rhs_scale=idle_scales[:],
+                    start=True,
+                    stop=True,
+                )
+
         ones = const.tile([P, P], BF16)
         nc.vector.memset(ones[:], 1.0)
         ident = const.tile([P, P], F32)
@@ -82,12 +101,12 @@ def tile_cross_module_pb_kernel(tc, q2, k1, v2, wc1, bc1, gamma2, x2, out):
         k1_col = const.tile([P, K_PASSES * PACK], F32)
         nc.vector.tensor_copy(out=k1_col[:], in_=k1_bf[:].rearrange("p a e -> p (a e)"))
         gamma_col = const.tile([P, 1], F32)
-        q2_cols = psum_agg.tile([P, M_CHUNK + 1], F32, tag="agg")
-        nc.tensor.matmul(out=q2_cols[:, 0:M_CHUNK], lhsT=ones[:], rhs=q2_row[:, 0:M_CHUNK], start=True, stop=True)
-        nc.tensor.matmul(
-            out=q2_cols[:, M_CHUNK : M_CHUNK + 1], lhsT=ones[:], rhs=q2_row[:, PIX : PIX + 1], start=True, stop=True
-        )
-        nc.vector.tensor_copy(out=gamma_col[:], in_=q2_cols[:, M_CHUNK : M_CHUNK + 1])
+        idle_passes(11)
+        q2_cols = psum_agg.tile([P, M_CHUNK], F32, tag="agg")
+        nc.tensor.matmul(out=q2_cols[:], lhsT=ones[:], rhs=q2_row[:, 0:M_CHUNK], start=True, stop=True)
+        gamma_bank = psum_z.tile([P, 1], F32, tag="z")
+        nc.tensor.matmul(out=gamma_bank[:], lhsT=ones[:], rhs=q2_row[:, PIX : PIX + 1], start=True, stop=True)
+        nc.vector.tensor_copy(out=gamma_col[:], in_=gamma_bank[:])
         gamma_bias = const.tile([P, O_TILES], F32)
         nc.vector.tensor_scalar(
             out=gamma_bias[:], in0=bias_bf[:], scalar1=gamma_col[:, 0:1], scalar2=None, op0=ALU.mult
@@ -135,13 +154,17 @@ def tile_cross_module_pb_kernel(tc, q2, k1, v2, wc1, bc1, gamma2, x2, out):
         def gate_first_sigmoid():
             for row in range(K_PASSES * PACK):
                 nc.scalar.activation(
-                    out=gate_rows[:, row, :], in_=q2_cols[:, 0:M_CHUNK], func=ACT.Sigmoid, scale=k1_col[:, row : row + 1]
+                    out=gate_rows[:, row, :], in_=q2_cols[:], func=ACT.Sigmoid, scale=k1_col[:, row : row + 1]
                 )
 
         def gate_first_interleave(g):
-            nc.vector.tensor_copy(
+            nc.gpsimd.tensor_scalar(
                 out=gate_grouped[0][:, g, :, :].rearrange("p (c i) t -> p c t i", i=4),
-                in_=gate_rows[:, g * PACK : (g + 1) * PACK, :].rearrange("p t (c i) -> p c t i", i=4),
+                in0=gate_rows[:, g * PACK : (g + 1) * PACK, :].rearrange("p t (c i) -> p c t i", i=4),
+                scalar1=1.0,
+                scalar2=0.0,
+                op0=ALU.mult,
+                op1=ALU.add,
             )
 
         logits = {}
@@ -301,41 +324,42 @@ def tile_cross_module_pb_kernel(tc, q2, k1, v2, wc1, bc1, gamma2, x2, out):
         gate_first_sigmoid()
         gate(2, 0)
         gate(2, 1)
-        for t in (0, 2):
-            for g in range(K_PASSES):
-                v2_transposes(t, g)
+        for g in range(K_PASSES):
+            v2_transposes(0, g)
+        idle_passes(4)
+        for g in range(K_PASSES):
+            v2_transposes(2, g)
         gate_first_interleave(0)
+        gate_first_interleave(1)
         v2_copy(dve_copy, 0, 0)
         v2_copy(act_copy, 2, 0)
         v2_copy(dve_copy, 0, 1)
         v2_copy(act_copy, 2, 1)
-        gate_first_interleave(1)
         gate(3, 0)
         gate(3, 1)
-        gate(4, 0)
-        gate(4, 1)
-        gate_quantise(0)
-        v2_quantise()
         for j in range(0, O_TILES, 2):
             w_transposes(j)
-        w_copy(act_copy, 4)
-        gate(5, 0)
+        gate_quantise(0)
+        v2_quantise()
+        gate(4, 0)
         agg_matmul(0)
         agg_copy(0)
+        gate(4, 1)
         agg_matmul(1)
         agg_copy(1)
-        w_copy(act_copy, 6)
-        gate(5, 1)
         w_copy(dve_copy, 0)
         w_copy(dve_copy, 2)
-        gate_quantise(1)
+        w_copy(act_copy, 4)
+        w_copy(act_copy, 6)
         w_quantise(0)
-        for j in range(0, O_TILES, 2):
-            bias_on_vector(j, slice(0, M_CHUNK))
-            bias_on_vector(j + 1, slice(0, M_CHUNK))
+        gate_quantise(1)
         agg_quantise(0)
+        for unit in (5,):
+            for g in range(K_PASSES):
+                gate(unit, g)
+        for j in range(O_TILES):
+            bias_on_vector(j, slice(0, M_CHUNK))
         w_quantise(1)
-        gate_quantise(2)
         for pair in range(pairs):
             if pair + 1 < pairs:
                 agg_matmul(2 * pair + 2)
@@ -348,17 +372,18 @@ def tile_cross_module_pb_kernel(tc, q2, k1, v2, wc1, bc1, gamma2, x2, out):
                 for unit in (6, 7):
                     for g in range(K_PASSES):
                         gate(unit, g)
-            if pair == 1:
-                for j in (0, 1, 2, 3, 4, 5, 6, 7):
-                    bias_on_scalar(j, slice(3 * M_CHUNK, PIX))
+            if 1 <= pair < pairs - 1:
+                for j in range(O_TILES):
+                    bias_on_scalar(j, slice((pair + 1) * M_CHUNK, (pair + 2) * M_CHUNK))
             y_finish(pair, 0)
             y_finish(pair, 2)
+            if pair == 0:
+                gate_quantise(2)
             if pair + 1 < pairs:
                 agg_quantise(pair + 1)
             y_finish(pair, 4)
             y_finish(pair, 6)
             if pair == 0:
                 gate_quantise(3)
-            if pair < 2:
                 for j in range(O_TILES):
-                    bias_on_vector(j, slice((pair + 1) * M_CHUNK, (pair + 2) * M_CHUNK))
+                    bias_on_vector(j, slice(M_CHUNK, 2 * M_CHUNK))

@@ -158,13 +158,9 @@ def tile_cross_module_pb_kernel(tc, q2, k1, v2, wc1, bc1, gamma2, x2, out):
                 )
 
         def gate_first_interleave(g):
-            nc.gpsimd.tensor_scalar(
+            nc.vector.tensor_copy(
                 out=gate_grouped[0][:, g, :, :].rearrange("p (c i) t -> p c t i", i=4),
-                in0=gate_rows[:, g * PACK : (g + 1) * PACK, :].rearrange("p t (c i) -> p c t i", i=4),
-                scalar1=1.0,
-                scalar2=0.0,
-                op0=ALU.mult,
-                op1=ALU.add,
+                in_=gate_rows[:, g * PACK : (g + 1) * PACK, :].rearrange("p t (c i) -> p c t i", i=4),
             )
 
         logits = {}
@@ -330,11 +326,11 @@ def tile_cross_module_pb_kernel(tc, q2, k1, v2, wc1, bc1, gamma2, x2, out):
         for g in range(K_PASSES):
             v2_transposes(2, g)
         gate_first_interleave(0)
-        gate_first_interleave(1)
         v2_copy(dve_copy, 0, 0)
         v2_copy(act_copy, 2, 0)
         v2_copy(dve_copy, 0, 1)
         v2_copy(act_copy, 2, 1)
+        gate_first_interleave(1)
         gate(3, 0)
         gate(3, 1)
         for j in range(0, O_TILES, 2):

@@ -75,25 +75,6 @@ def tile_cross_module_pb_kernel(tc, q2, k1, v2, wc1, bc1, gamma2, x2, out):
         table_out = const.tile([P, 1], F32)
         nc.scalar.activation(out=table_out[:], in_=table_probe[:], func=ACT.Sigmoid)
 
-        idle_grouped = const.tile([P, PACK * P], BF16, align_bytes=64)
-        nc.vector.memset(idle_grouped[:].bitcast(U32), 0)
-        idle_codes = const.tile([P, P], U32, align_bytes=64)
-        idle_scales = const.tile([P, P], U8, align_bytes=64)
-        nc.vector.quantize_mx(out=idle_codes[:].bitcast(FP8X4), scales=idle_scales[:], in_=idle_grouped[:])
-        idle_bank = psum_agg.tile([P, P], F32, tag="agg")
-
-        def idle_passes(count):
-            for repeat in range(count):
-                nc.tensor.matmul_mx(
-                    out=idle_bank[:],
-                    lhsT=idle_codes[:].bitcast(FP8X4),
-                    lhsT_scale=idle_scales[:],
-                    rhs=idle_codes[:].bitcast(FP8X4),
-                    rhs_scale=idle_scales[:],
-                    start=True,
-                    stop=True,
-                )
-
         ones = const.tile([P, P], BF16)
         nc.vector.memset(ones[:], 1.0)
         ident = const.tile([P, P], F32)
@@ -101,7 +82,6 @@ def tile_cross_module_pb_kernel(tc, q2, k1, v2, wc1, bc1, gamma2, x2, out):
         k1_col = const.tile([P, K_PASSES * PACK], F32)
         nc.vector.tensor_copy(out=k1_col[:], in_=k1_bf[:].rearrange("p a e -> p (a e)"))
         gamma_col = const.tile([P, 1], F32)
-        idle_passes(11)
         q2_cols = psum_agg.tile([P, M_CHUNK], F32, tag="agg")
         nc.tensor.matmul(out=q2_cols[:], lhsT=ones[:], rhs=q2_row[:, 0:M_CHUNK], start=True, stop=True)
         gamma_bank = psum_z.tile([P, 1], F32, tag="z")
@@ -322,7 +302,6 @@ def tile_cross_module_pb_kernel(tc, q2, k1, v2, wc1, bc1, gamma2, x2, out):
         gate(2, 1)
         for g in range(K_PASSES):
             v2_transposes(0, g)
-        idle_passes(4)
         for g in range(K_PASSES):
             v2_transposes(2, g)
         gate_first_interleave(0)

@@ -43,19 +43,26 @@ def tile_cross_module_pb_kernel(tc, q2, k1, v2, wc1, bc1, gamma2, x2, out):
         psum_wide = ctx.enter_context(tc.psum_pool(name="psum_wide", bufs=4))
         ctx.enter_context(tc.manual_schedule())
 
-        q2_row = const.tile([P, PIX + 2], BF16)
-        nc.vector.memset(q2_row[:].bitcast(U32), 0)
-        k1_row = const.tile([P, PIX], BF16)
-        nc.gpsimd.memset(k1_row[:].bitcast(U32), 0)
+        q2_first = const.tile([P, M_CHUNK + 2], BF16)
+        nc.vector.memset(q2_first[:].bitcast(U32), 0)
+        table_probe = const.tile([P, 1], F32)
+        nc.vector.memset(table_probe[:], 0.0)
+        k1_rows = const.tile([P, K_PASSES, 2 * P], BF16)
+        nc.vector.memset(k1_rows[:].rearrange("q g x -> q (g x)").bitcast(U32), 0)
+        q2_rows = const.tile([P, PIX - M_CHUNK], BF16)
+        nc.vector.memset(q2_rows[:].bitcast(U32), 0)
         k1_bf = const.tile([P, K_PASSES * 2, 2], BF16)
         nc.sync.dma_start(out=k1_bf[:], in_=k1.rearrange("b (a p e) -> p (b a) e", p=P, e=2))
-        nc.sync.dma_start(out=k1_row[0:1, :], in_=k1)
-        nc.sync.dma_start(out=q2_row[0:1, 0:PIX], in_=q2)
-        nc.sync.dma_start(out=q2_row[0:1, PIX : PIX + 1], in_=gamma2.rearrange("(a b) -> a b", a=1))
+        nc.sync.dma_start(out=q2_first[0:1, 0:M_CHUNK], in_=q2[:, 0:M_CHUNK])
+        k1_runs = k1.rearrange("b (g u x) -> (b u) g x", u=2, x=2 * P)
+        for e in range(2):
+            nc.sync.dma_start(out=k1_rows[2 * e : 2 * e + 2, :, 0 : 2 * P - e], in_=k1_runs[:, :, e : 2 * P])
+        nc.sync.dma_start(out=q2_rows[0:PACK, :], in_=q2[:, M_CHUNK:PIX].partition_broadcast(PACK))
         v2_sb = keep.tile([P, C_TILES, PIX], BF16)
         v2_rows = v2.rearrange("b (u r e) k -> (b u) r e k", r=P, e=2)
-        for u in range(2):
-            nc.sync.dma_start(out=v2_sb[:, 2 * u : 2 * u + 2, :], in_=v2_rows[u])
+        nc.sync.dma_start(out=v2_sb[:, 0:2, :], in_=v2_rows[0])
+        nc.sync.dma_start(out=v2_sb[:, 2:4, :], in_=v2_rows[1])
+        nc.sync.dma_start(out=q2_first[0:1, M_CHUNK : M_CHUNK + 1], in_=gamma2.rearrange("(a b) -> a b", a=1))
         w_sb = keep.tile([P, O_TILES, C_IN], BF16)
         w_rows = wc1.rearrange("(r j) c -> r j c", j=O_TILES)
         for half in range(2):
@@ -70,8 +77,6 @@ def tile_cross_module_pb_kernel(tc, q2, k1, v2, wc1, bc1, gamma2, x2, out):
         bias_bf = const.tile([P, O_TILES], BF16)
         nc.scalar.dma_start(out=bias_bf[:], in_=bc1.rearrange("(r j) -> r j", j=O_TILES))
 
-        table_probe = const.tile([P, 1], F32)
-        nc.vector.memset(table_probe[:], 0.0)
         table_out = const.tile([P, 1], F32)
         nc.scalar.activation(out=table_out[:], in_=table_probe[:], func=ACT.Sigmoid)
 
@@ -82,24 +87,24 @@ def tile_cross_module_pb_kernel(tc, q2, k1, v2, wc1, bc1, gamma2, x2, out):
         k1_col = const.tile([P, K_PASSES * PACK], F32)
         nc.vector.tensor_copy(out=k1_col[:], in_=k1_bf[:].rearrange("p a e -> p (a e)"))
         gamma_col = const.tile([P, 1], F32)
-        q2_cols = psum_agg.tile([P, M_CHUNK], F32, tag="agg")
-        nc.tensor.matmul(out=q2_cols[:], lhsT=ones[:], rhs=q2_row[:, 0:M_CHUNK], start=True, stop=True)
-        gamma_bank = psum_z.tile([P, 1], F32, tag="z")
-        nc.tensor.matmul(out=gamma_bank[:], lhsT=ones[:], rhs=q2_row[:, PIX : PIX + 1], start=True, stop=True)
-        nc.vector.tensor_copy(out=gamma_col[:], in_=gamma_bank[:])
         gamma_bias = const.tile([P, O_TILES], F32)
-        nc.vector.tensor_scalar(
-            out=gamma_bias[:], in0=bias_bf[:], scalar1=gamma_col[:, 0:1], scalar2=None, op0=ALU.mult
-        )
-        k1_stat = const.tile([P, K_PASSES * PACK, P], BF16)
-        nc.gpsimd.tensor_scalar(
-            out=k1_stat[:].rearrange("q (a e) p -> q a e p", e=2),
-            in0=k1_row[:].rearrange("q (a p e) -> q a e p", p=P, e=2),
-            scalar1=1.0,
-            scalar2=0.0,
-            op0=ALU.mult,
-            op1=ALU.add,
-        )
+        q2_cols = psum_agg.tile([P, M_CHUNK], F32, tag="agg")
+        nc.tensor.matmul(out=q2_cols[:], lhsT=ones[:], rhs=q2_first[:, 0:M_CHUNK], start=True, stop=True)
+        k1_stat = const.tile([P, K_PASSES, P], BF16)
+        nc.vector.tensor_copy(out=k1_stat[:], in_=k1_rows[:].rearrange("q g (p e) -> q g p e", e=2)[:, :, :, 0])
+
+        units = PIX // M_SUB
+        first_units = M_CHUNK // M_SUB
+        q2_blocks = const.tile([P, units - first_units, PACK, M_SUB], BF16)
+        for u in range(2):
+            for e in range(2):
+                nc.vector.tensor_scalar(
+                    out=q2_blocks[:, :, 2 * u + e, :],
+                    in0=q2_rows[:].rearrange("q (n m) -> q n m", m=M_SUB),
+                    scalar1=ident[:, 2 * e + u : 2 * e + u + 1],
+                    scalar2=None,
+                    op0=ALU.mult,
+                )
 
         x2_biased = keep.tile([P, O_TILES, PIX], F32)
 
@@ -147,14 +152,13 @@ def tile_cross_module_pb_kernel(tc, q2, k1, v2, wc1, bc1, gamma2, x2, out):
 
         def gate_logits(unit, g):
             z_bank = psum_z.tile([P, PACK, M_SUB], F32, tag="z")
-            for t in range(PACK):
-                nc.tensor.matmul(
-                    out=z_bank[:, t, :],
-                    lhsT=k1_stat[:, g * PACK + t, :],
-                    rhs=q2_row[:, unit * M_SUB : (unit + 1) * M_SUB],
-                    start=True,
-                    stop=True,
-                )
+            nc.tensor.matmul(
+                out=z_bank[:].rearrange("p t m -> p (t m)"),
+                lhsT=k1_stat[:, g, :],
+                rhs=q2_blocks[:, unit - first_units, :, :].rearrange("q t m -> q (t m)"),
+                start=True,
+                stop=True,
+            )
             logits[unit, g] = z_bank
 
         def gate_sigmoid(unit, g):
@@ -163,6 +167,16 @@ def tile_cross_module_pb_kernel(tc, q2, k1, v2, wc1, bc1, gamma2, x2, out):
                 out=gate_grouped[pair][:, g, sub * M_SUB : (sub + 1) * M_SUB, :],
                 in_=logits[unit, g][:].rearrange("p t m -> p m t"),
                 func=ACT.Sigmoid,
+            )
+
+        def spread_gamma():
+            gamma_bank = psum_wide.tile([P, 1], F32, tag="wide")
+            nc.tensor.matmul(
+                out=gamma_bank[:], lhsT=ones[:], rhs=q2_first[:, M_CHUNK : M_CHUNK + 1], start=True, stop=True
+            )
+            nc.vector.tensor_copy(out=gamma_col[:], in_=gamma_bank[:])
+            nc.vector.tensor_scalar(
+                out=gamma_bias[:], in0=bias_bf[:], scalar1=gamma_col[:, 0:1], scalar2=None, op0=ALU.mult
             )
 
         def gate_quantise(pair):
@@ -298,18 +312,19 @@ def tile_cross_module_pb_kernel(tc, q2, k1, v2, wc1, bc1, gamma2, x2, out):
             gate_sigmoid(unit, g)
 
         gate_first_sigmoid()
+        for g in range(K_PASSES):
+            v2_transposes(0, g)
         gate(2, 0)
         gate(2, 1)
         for g in range(K_PASSES):
-            v2_transposes(0, g)
-        for g in range(K_PASSES):
             v2_transposes(2, g)
-        gate_first_interleave(0)
         v2_copy(dve_copy, 0, 0)
+        gate_first_interleave(0)
         v2_copy(act_copy, 2, 0)
         v2_copy(dve_copy, 0, 1)
         v2_copy(act_copy, 2, 1)
         gate_first_interleave(1)
+        spread_gamma()
         gate(3, 0)
         gate(3, 1)
         for j in range(0, O_TILES, 2):

@@ -37,7 +37,7 @@ def tile_cross_module_pb_kernel(tc, q2, k1, v2, wc1, bc1, gamma2, x2, out):
         const = ctx.enter_context(tc.tile_pool(name="const", bufs=1))
         keep = ctx.enter_context(tc.tile_pool(name="keep", bufs=1))
         work = ctx.enter_context(tc.tile_pool(name="work", bufs=4))
-        result = ctx.enter_context(tc.tile_pool(name="result", bufs=6))
+        result = ctx.enter_context(tc.tile_pool(name="result", bufs=16))
         psum_z = ctx.enter_context(tc.psum_pool(name="psum_z", bufs=2))
         psum_agg = ctx.enter_context(tc.psum_pool(name="psum_agg", bufs=2))
         psum_wide = ctx.enter_context(tc.psum_pool(name="psum_wide", bufs=4))
@@ -51,16 +51,14 @@ def tile_cross_module_pb_kernel(tc, q2, k1, v2, wc1, bc1, gamma2, x2, out):
         nc.vector.memset(k1_rows[:].rearrange("q g x -> q (g x)").bitcast(U32), 0)
         q2_rows = const.tile([P, PIX - M_CHUNK], BF16)
         nc.vector.memset(q2_rows[:].bitcast(U32), 0)
-        k1_bf = const.tile([P, K_PASSES * 2, 2], BF16)
-        nc.sync.dma_start(out=k1_bf[:], in_=k1.rearrange("b (a p e) -> p (b a) e", p=P, e=2))
         nc.sync.dma_start(out=q2_first[0:1, 0:M_CHUNK], in_=q2[:, 0:M_CHUNK])
         k1_runs = k1.rearrange("b (g u x) -> (b u) g x", u=2, x=2 * P)
         for e in range(2):
             nc.sync.dma_start(out=k1_rows[2 * e : 2 * e + 2, :, 0 : 2 * P - e], in_=k1_runs[:, :, e : 2 * P])
-        nc.sync.dma_start(out=q2_rows[0:PACK, :], in_=q2[:, M_CHUNK:PIX].partition_broadcast(PACK))
         v2_sb = keep.tile([P, C_TILES, PIX], BF16)
         v2_rows = v2.rearrange("b (u r e) k -> (b u) r e k", r=P, e=2)
         nc.sync.dma_start(out=v2_sb[:, 0:2, :], in_=v2_rows[0])
+        nc.sync.dma_start(out=q2_rows[0:PACK, :], in_=q2[:, M_CHUNK:PIX].partition_broadcast(PACK))
         nc.sync.dma_start(out=v2_sb[:, 2:4, :], in_=v2_rows[1])
         nc.sync.dma_start(out=q2_first[0:1, M_CHUNK : M_CHUNK + 1], in_=gamma2.rearrange("(a b) -> a b", a=1))
         w_sb = keep.tile([P, O_TILES, C_IN], BF16)
@@ -74,6 +72,8 @@ def tile_cross_module_pb_kernel(tc, q2, k1, v2, wc1, bc1, gamma2, x2, out):
             m_half = slice(half * PIX // 2, (half + 1) * PIX // 2)
             nc.sync.dma_start(out=x2_sb[:, :, m_half], in_=x2_rows[:, :, m_half])
         out_rows = out.rearrange("b (r j) h w -> r (b j) (h w)", j=O_TILES)
+        k1_bf = const.tile([P, K_PASSES * 2, 2], BF16)
+        nc.scalar.dma_start(out=k1_bf[:], in_=k1.rearrange("b (a p e) -> p (b a) e", p=P, e=2))
         bias_bf = const.tile([P, O_TILES], BF16)
         nc.scalar.dma_start(out=bias_bf[:], in_=bc1.rearrange("(r j) -> r j", j=O_TILES))
 
@@ -96,6 +96,7 @@ def tile_cross_module_pb_kernel(tc, q2, k1, v2, wc1, bc1, gamma2, x2, out):
         units = PIX // M_SUB
         first_units = M_CHUNK // M_SUB
         q2_blocks = const.tile([P, units - first_units, PACK, M_SUB], BF16)
+
         for u in range(2):
             for e in range(2):
                 nc.vector.tensor_scalar(
@@ -174,6 +175,9 @@ def tile_cross_module_pb_kernel(tc, q2, k1, v2, wc1, bc1, gamma2, x2, out):
             nc.tensor.matmul(
                 out=gamma_bank[:], lhsT=ones[:], rhs=q2_first[:, M_CHUNK : M_CHUNK + 1], start=True, stop=True
             )
+            return gamma_bank
+
+        def gamma_constants(gamma_bank):
             nc.vector.tensor_copy(out=gamma_col[:], in_=gamma_bank[:])
             nc.vector.tensor_scalar(
                 out=gamma_bias[:], in0=bias_bf[:], scalar1=gamma_col[:, 0:1], scalar2=None, op0=ALU.mult
@@ -318,37 +322,38 @@ def tile_cross_module_pb_kernel(tc, q2, k1, v2, wc1, bc1, gamma2, x2, out):
         gate(2, 1)
         for g in range(K_PASSES):
             v2_transposes(2, g)
-        v2_copy(dve_copy, 0, 0)
         gate_first_interleave(0)
+        v2_copy(dve_copy, 0, 0)
         v2_copy(act_copy, 2, 0)
         v2_copy(dve_copy, 0, 1)
         v2_copy(act_copy, 2, 1)
         gate_first_interleave(1)
-        spread_gamma()
+        gamma_bank = spread_gamma()
+        gate_quantise(0)
+        gamma_constants(gamma_bank)
+        v2_quantise()
         gate(3, 0)
         gate(3, 1)
-        for j in range(0, O_TILES, 2):
+        for j in (0, 2, 4):
             w_transposes(j)
-        gate_quantise(0)
-        v2_quantise()
+        w_copy(act_copy, 4)
         gate(4, 0)
         agg_matmul(0)
         agg_copy(0)
+        w_copy(dve_copy, 0)
         gate(4, 1)
         agg_matmul(1)
         agg_copy(1)
-        w_copy(dve_copy, 0)
+        w_transposes(6)
         w_copy(dve_copy, 2)
-        w_copy(act_copy, 4)
-        w_copy(act_copy, 6)
-        w_quantise(0)
         gate_quantise(1)
-        agg_quantise(0)
-        for unit in (5,):
-            for g in range(K_PASSES):
-                gate(unit, g)
+        w_copy(act_copy, 6)
+        for g in range(K_PASSES):
+            gate(5, g)
         for j in range(O_TILES):
             bias_on_vector(j, slice(0, M_CHUNK))
+        w_quantise(0)
+        agg_quantise(0)
         w_quantise(1)
         for pair in range(pairs):
             if pair + 1 < pairs:
@@ -358,6 +363,9 @@ def tile_cross_module_pb_kernel(tc, q2, k1, v2, wc1, bc1, gamma2, x2, out):
                 agg_copy(2 * pair + 3)
             for j in (0, 2, 4, 6):
                 y_matmul(pair, j)
+            if pair == 0:
+                for j in range(O_TILES // 2):
+                    bias_on_vector(j, slice(M_CHUNK, 2 * M_CHUNK))
             if pair == 0:
                 for unit in (6, 7):
                     for g in range(K_PASSES):
@@ -369,11 +377,11 @@ def tile_cross_module_pb_kernel(tc, q2, k1, v2, wc1, bc1, gamma2, x2, out):
             y_finish(pair, 2)
             if pair == 0:
                 gate_quantise(2)
+            y_finish(pair, 4)
             if pair + 1 < pairs:
                 agg_quantise(pair + 1)
-            y_finish(pair, 4)
             y_finish(pair, 6)
             if pair == 0:
-                gate_quantise(3)
-                for j in range(O_TILES):
+                for j in range(O_TILES // 2, O_TILES):
                     bias_on_vector(j, slice(M_CHUNK, 2 * M_CHUNK))
+                gate_quantise(3)

from contextlib import ExitStack

from concourse import mybir
from concourse.masks import make_identity

F32 = mybir.dt.float32
BF16 = mybir.dt.bfloat16
U32 = mybir.dt.uint32
U8 = mybir.dt.uint8
FP8X4 = mybir.dt.float8_e4m3fn_x4
ACT = mybir.ActivationFunctionType
ALU = mybir.AluOpType

P = 128
PACK = 4
PIX = 1024
C_IN = 512
C_OUT = 1024
K_PASSES = PIX // (P * PACK)
C_TILES = C_IN // P
O_TILES = C_OUT // P
BANK = 512
M_CHUNK = 256
M_SUB = BANK // C_TILES

FLOPS = 2 * C_IN * PIX * PIX + 2 * C_OUT * C_IN * PIX


def word_view(grouped):
    flat = grouped.rearrange("p c t -> p (c t)").bitcast(F32)
    return flat.rearrange("p (c u) -> p c u", u=2)


def tile_cross_module_pb_kernel(tc, q2, k1, v2, wc1, bc1, gamma2, x2, out):
    nc = tc.nc
    with ExitStack() as ctx:
        const = ctx.enter_context(tc.tile_pool(name="const", bufs=1))
        keep = ctx.enter_context(tc.tile_pool(name="keep", bufs=1))
        work = ctx.enter_context(tc.tile_pool(name="work", bufs=4))
        result = ctx.enter_context(tc.tile_pool(name="result", bufs=16))
        psum_z = ctx.enter_context(tc.psum_pool(name="psum_z", bufs=2))
        psum_agg = ctx.enter_context(tc.psum_pool(name="psum_agg", bufs=2))
        psum_wide = ctx.enter_context(tc.psum_pool(name="psum_wide", bufs=4))
        ctx.enter_context(tc.manual_schedule())

        q2_first = const.tile([P, M_CHUNK + 2], BF16)
        nc.vector.memset(q2_first[:].bitcast(U32), 0)
        table_probe = const.tile([P, 1], F32)
        nc.vector.memset(table_probe[:], 0.0)
        k1_rows = const.tile([P, K_PASSES, 2 * P], BF16)
        nc.vector.memset(k1_rows[:].rearrange("q g x -> q (g x)").bitcast(U32), 0)
        q2_rows = const.tile([P, PIX - M_CHUNK], BF16)
        nc.vector.memset(q2_rows[:].bitcast(U32), 0)
        nc.sync.dma_start(out=q2_first[0:1, 0:M_CHUNK], in_=q2[:, 0:M_CHUNK])
        k1_runs = k1.rearrange("b (g u x) -> (b u) g x", u=2, x=2 * P)
        for e in range(2):
            nc.sync.dma_start(out=k1_rows[2 * e : 2 * e + 2, :, 0 : 2 * P - e], in_=k1_runs[:, :, e : 2 * P])
        v2_sb = keep.tile([P, C_TILES, PIX], BF16)
        v2_rows = v2.rearrange("b (u r e) k -> (b u) r e k", r=P, e=2)
        nc.sync.dma_start(out=v2_sb[:, 0:2, :], in_=v2_rows[0])
        nc.sync.dma_start(out=q2_rows[0:PACK, :], in_=q2[:, M_CHUNK:PIX].partition_broadcast(PACK))
        nc.sync.dma_start(out=v2_sb[:, 2:4, :], in_=v2_rows[1])
        nc.sync.dma_start(out=q2_first[0:1, M_CHUNK : M_CHUNK + 1], in_=gamma2.rearrange("(a b) -> a b", a=1))
        w_sb = keep.tile([P, O_TILES, C_IN], BF16)
        w_rows = wc1.rearrange("(r j) c -> r j c", j=O_TILES)
        for half in range(2):
            j_half = slice(half * O_TILES // 2, (half + 1) * O_TILES // 2)
            nc.sync.dma_start(out=w_sb[:, j_half, :], in_=w_rows[:, j_half, :])
        x2_sb = keep.tile([P, O_TILES, PIX], BF16)
        x2_rows = x2.rearrange("b (r j) h w -> r (b j) (h w)", j=O_TILES)
        for half in range(2):
            m_half = slice(half * PIX // 2, (half + 1) * PIX // 2)
            nc.sync.dma_start(out=x2_sb[:, :, m_half], in_=x2_rows[:, :, m_half])
        out_rows = out.rearrange("b (r j) h w -> r (b j) (h w)", j=O_TILES)
        k1_bf = const.tile([P, K_PASSES * 2, 2], BF16)
        nc.scalar.dma_start(out=k1_bf[:], in_=k1.rearrange("b (a p e) -> p (b a) e", p=P, e=2))
        bias_bf = const.tile([P, O_TILES], BF16)
        nc.scalar.dma_start(out=bias_bf[:], in_=bc1.rearrange("(r j) -> r j", j=O_TILES))

        table_out = const.tile([P, 1], F32)
        nc.scalar.activation(out=table_out[:], in_=table_probe[:], func=ACT.Sigmoid)

        ones = const.tile([P, P], BF16)
        nc.vector.memset(ones[:], 1.0)
        ident = const.tile([P, P], F32)
        make_identity(nc, ident[:])
        k1_col = const.tile([P, K_PASSES * PACK], F32)
        nc.vector.tensor_copy(out=k1_col[:], in_=k1_bf[:].rearrange("p a e -> p (a e)"))
        gamma_col = const.tile([P, 1], F32)
        gamma_bias = const.tile([P, O_TILES], F32)
        q2_cols = psum_agg.tile([P, M_CHUNK], F32, tag="agg")
        nc.tensor.matmul(out=q2_cols[:], lhsT=ones[:], rhs=q2_first[:, 0:M_CHUNK], start=True, stop=True)
        k1_stat = const.tile([P, K_PASSES, P], BF16)
        nc.vector.tensor_copy(out=k1_stat[:], in_=k1_rows[:].rearrange("q g (p e) -> q g p e", e=2)[:, :, :, 0])

        units = PIX // M_SUB
        first_units = M_CHUNK // M_SUB
        q2_blocks = const.tile([P, units - first_units, PACK, M_SUB], BF16)

        for u in range(2):
            for e in range(2):
                nc.vector.tensor_scalar(
                    out=q2_blocks[:, :, 2 * u + e, :],
                    in0=q2_rows[:].rearrange("q (n m) -> q n m", m=M_SUB),
                    scalar1=ident[:, 2 * e + u : 2 * e + u + 1],
                    scalar2=None,
                    op0=ALU.mult,
                )

        x2_biased = keep.tile([P, O_TILES, PIX], F32)

        def bias_on_vector(j, m_cols):
            nc.vector.tensor_scalar(
                out=x2_biased[:, j, m_cols],
                in0=x2_sb[:, j, m_cols],
                scalar1=gamma_bias[:, j : j + 1],
                scalar2=None,
                op0=ALU.add,
            )

        def bias_on_scalar(j, m_cols):
            nc.scalar.activation(
                out=x2_biased[:, j, m_cols],
                in_=x2_sb[:, j, m_cols],
                func=ACT.Identity,
                bias=gamma_bias[:, j : j + 1],
            )

        pairs = PIX // M_CHUNK
        subs = M_CHUNK // M_SUB
        gate_grouped = [work.tile([P, K_PASSES, M_CHUNK, PACK], BF16, name="gate_grouped", align_bytes=64) for p in range(pairs)]
        gate_codes = [work.tile([P, K_PASSES, M_CHUNK], U32, name="gate_codes", align_bytes=64) for p in range(pairs)]
        gate_scales = [work.tile([P, K_PASSES, M_CHUNK], U8, name="gate_scales", align_bytes=64) for p in range(pairs)]
        agg_grouped = [work.tile([P, M_CHUNK, PACK], BF16, name="agg_grouped", align_bytes=64) for p in range(pairs)]
        agg_codes = [work.tile([P, M_CHUNK], U32, name="agg_codes", align_bytes=64) for p in range(pairs)]
        agg_scales = [work.tile([P, M_CHUNK], U8, name="agg_scales", align_bytes=64) for p in range(pairs)]

        gate_rows = keep.tile([P, K_PASSES * PACK, M_CHUNK], BF16)

        def gate_first_sigmoid():
            for row in range(K_PASSES * PACK):
                nc.scalar.activation(
                    out=gate_rows[:, row, :], in_=q2_cols[:], func=ACT.Sigmoid, scale=k1_col[:, row : row + 1]
                )

        def gate_first_interleave(g):
            nc.vector.tensor_copy(
                out=gate_grouped[0][:, g, :, :].rearrange("p (c i) t -> p c t i", i=4),
                in_=gate_rows[:, g * PACK : (g + 1) * PACK, :].rearrange("p t (c i) -> p c t i", i=4),
            )

        logits = {}

        def gate_logits(unit, g):
            z_bank = psum_z.tile([P, PACK, M_SUB], F32, tag="z")
            nc.tensor.matmul(
                out=z_bank[:].rearrange("p t m -> p (t m)"),
                lhsT=k1_stat[:, g, :],
                rhs=q2_blocks[:, unit - first_units, :, :].rearrange("q t m -> q (t m)"),
                start=True,
                stop=True,
            )
            logits[unit, g] = z_bank

        def gate_sigmoid(unit, g):
            pair, sub = divmod(unit, subs)
            nc.scalar.activation(
                out=gate_grouped[pair][:, g, sub * M_SUB : (sub + 1) * M_SUB, :],
                in_=logits[unit, g][:].rearrange("p t m -> p m t"),
                func=ACT.Sigmoid,
            )

        def spread_gamma():
            gamma_bank = psum_wide.tile([P, 1], F32, tag="wide")
            nc.tensor.matmul(
                out=gamma_bank[:], lhsT=ones[:], rhs=q2_first[:, M_CHUNK : M_CHUNK + 1], start=True, stop=True
            )
            return gamma_bank

        def gamma_constants(gamma_bank):
            nc.vector.tensor_copy(out=gamma_col[:], in_=gamma_bank[:])
            nc.vector.tensor_scalar(
                out=gamma_bias[:], in0=bias_bf[:], scalar1=gamma_col[:, 0:1], scalar2=None, op0=ALU.mult
            )

        def gate_quantise(pair):
            for g in range(K_PASSES):
                nc.vector.quantize_mx(
                    out=gate_codes[pair][:, g, :].bitcast(FP8X4),
                    scales=gate_scales[pair][:, g, :],
                    in_=gate_grouped[pair][:, g, :, :].rearrange("p m t -> p (m t)"),
                )

        def transpose_two_tiles(rows_sb, first_tile, word_base):
            flipped = psum_wide.tile([P, 2, 2 * P], F32, tag="wide")
            for i in range(2):
                for u in range(2):
                    words = rows_sb[:, first_tile + i, :].bitcast(F32)
                    nc.tensor.transpose(
                        flipped[:, u, i * P : (i + 1) * P],
                        words[:, word_base + u * P : word_base + (u + 1) * P],
                        ident[:],
                    )
            return flipped

        def lay_words(copy, flipped, grouped_cols):
            copy(out=word_view(grouped_cols), in_=flipped[:].rearrange("p u r -> p r u"))

        v2_grouped = keep.tile([P, K_PASSES, C_IN, PACK], BF16, align_bytes=64)
        v2_codes = keep.tile([P, K_PASSES, C_IN], U32, align_bytes=64)
        v2_scales = keep.tile([P, K_PASSES, C_IN], U8, align_bytes=64)
        w_grouped = keep.tile([P, C_OUT, PACK], BF16, align_bytes=64)
        w_codes = keep.tile([P, C_OUT], U32, align_bytes=64)
        w_scales = keep.tile([P, C_OUT], U8, align_bytes=64)

        flipped_v2 = {}

        def v2_transposes(t, g):
            flipped_v2[t, g] = transpose_two_tiles(v2_sb, t, g * 2 * P)

        def v2_copy(copy, t, g):
            lay_words(copy, flipped_v2[t, g], v2_grouped[:, g, t * P : (t + 2) * P, :])

        flipped_w = {}

        def w_transposes(j):
            flipped_w[j] = transpose_two_tiles(w_sb, j, 0)

        def w_copy(copy, j):
            lay_words(copy, flipped_w[j], w_grouped[:, j * P : (j + 2) * P, :])

        def v2_quantise():
            for g in range(K_PASSES):
                nc.vector.quantize_mx(
                    out=v2_codes[:, g, :].bitcast(FP8X4),
                    scales=v2_scales[:, g, :],
                    in_=v2_grouped[:, g, :, :].rearrange("p c t -> p (c t)"),
                )

        def w_quantise(half):
            o_half = slice(half * C_OUT // 2, (half + 1) * C_OUT // 2)
            nc.vector.quantize_mx(
                out=w_codes[:, o_half].bitcast(FP8X4),
                scales=w_scales[:, o_half],
                in_=w_grouped[:, o_half, :].rearrange("p o t -> p (o t)"),
            )

        agg_banks = {}

        def agg_matmul(unit):
            pair, sub = divmod(unit, subs)
            m_sub = slice(sub * M_SUB, (sub + 1) * M_SUB)
            agg_bank = psum_agg.tile([P, C_TILES, M_SUB], F32, tag="agg")
            for t in range(C_TILES):
                c_cols = slice(t * P, (t + 1) * P)
                for g in range(K_PASSES):
                    nc.tensor.matmul_mx(
                        out=agg_bank[:, t, :],
                        lhsT=v2_codes[:, g, c_cols].bitcast(FP8X4),
                        lhsT_scale=v2_scales[:, g, c_cols],
                        rhs=gate_codes[pair][:, g, m_sub].bitcast(FP8X4),
                        rhs_scale=gate_scales[pair][:, g, m_sub],
                        start=(g == 0),
                        stop=(g == K_PASSES - 1),
                    )
            agg_banks[unit] = agg_bank

        def agg_copy(unit):
            pair, sub = divmod(unit, subs)
            nc.scalar.copy(
                out=agg_grouped[pair][:, sub * M_SUB : (sub + 1) * M_SUB, :],
                in_=agg_banks[unit][:].rearrange("p t m -> p m t"),
            )

        def agg_quantise(pair):
            nc.vector.quantize_mx(
                out=agg_codes[pair][:].bitcast(FP8X4),
                scales=agg_scales[pair][:],
                in_=agg_grouped[pair][:].rearrange("p m t -> p (m t)"),
            )

        y_psum = {}

        def y_matmul(pair, j):
            y_bank = psum_wide.tile([P, 2, M_CHUNK], F32, tag="wide")
            for i in range(2):
                o_cols = slice((j + i) * P, (j + i + 1) * P)
                nc.tensor.matmul_mx(
                    out=y_bank[:, i, :],
                    lhsT=w_codes[:, o_cols].bitcast(FP8X4),
                    lhsT_scale=w_scales[:, o_cols],
                    rhs=agg_codes[pair][:].bitcast(FP8X4),
                    rhs_scale=agg_scales[pair][:],
                    start=True,
                    stop=True,
                )
            y_psum[pair, j] = y_bank

        def y_finish(pair, j):
            m_cols = slice(pair * M_CHUNK, (pair + 1) * M_CHUNK)
            out_sb = result.tile([P, 2, M_CHUNK], F32, name="out_sb")
            nc.vector.scalar_tensor_tensor(
                out=out_sb[:],
                in0=y_psum[pair, j][:],
                scalar=gamma_col[:, 0:1],
                in1=x2_biased[:, j : j + 2, m_cols],
                op0=ALU.mult,
                op1=ALU.add,
            )
            nc.sync.dma_start(out=out_rows[:, j : j + 2, m_cols], in_=out_sb[:])

        dve_copy, act_copy = nc.vector.tensor_copy, nc.scalar.copy

        def gate(unit, g):
            gate_logits(unit, g)
            gate_sigmoid(unit, g)

        gate_first_sigmoid()
        for g in range(K_PASSES):
            v2_transposes(0, g)
        gate(2, 0)
        gate(2, 1)
        for g in range(K_PASSES):
            v2_transposes(2, g)
        gate_first_interleave(0)
        v2_copy(dve_copy, 0, 0)
        v2_copy(act_copy, 2, 0)
        v2_copy(dve_copy, 0, 1)
        v2_copy(act_copy, 2, 1)
        gate_first_interleave(1)
        gamma_bank = spread_gamma()
        gate_quantise(0)
        gamma_constants(gamma_bank)
        v2_quantise()
        gate(3, 0)
        gate(3, 1)
        for j in (0, 2, 4):
            w_transposes(j)
        w_copy(act_copy, 4)
        gate(4, 0)
        agg_matmul(0)
        agg_copy(0)
        w_copy(dve_copy, 0)
        gate(4, 1)
        agg_matmul(1)
        agg_copy(1)
        w_transposes(6)
        w_copy(dve_copy, 2)
        gate_quantise(1)
        w_copy(act_copy, 6)
        for g in range(K_PASSES):
            gate(5, g)
        for j in range(O_TILES):
            bias_on_vector(j, slice(0, M_CHUNK))
        w_quantise(0)
        agg_quantise(0)
        w_quantise(1)
        for pair in range(pairs):
            if pair + 1 < pairs:
                agg_matmul(2 * pair + 2)
                agg_copy(2 * pair + 2)
                agg_matmul(2 * pair + 3)
                agg_copy(2 * pair + 3)
            for j in (0, 2, 4, 6):
                y_matmul(pair, j)
            if pair == 0:
                for j in range(O_TILES // 2):
                    bias_on_vector(j, slice(M_CHUNK, 2 * M_CHUNK))
            if pair == 0:
                for unit in (6, 7):
                    for g in range(K_PASSES):
                        gate(unit, g)
            if 1 <= pair < pairs - 1:
                for j in range(O_TILES):
                    bias_on_scalar(j, slice((pair + 1) * M_CHUNK, (pair + 2) * M_CHUNK))
            y_finish(pair, 0)
            y_finish(pair, 2)
            if pair == 0:
                gate_quantise(2)
            y_finish(pair, 4)
            if pair + 1 < pairs:
                agg_quantise(pair + 1)
            y_finish(pair, 6)
            if pair == 0:
                for j in range(O_TILES // 2, O_TILES):
                    bias_on_vector(j, slice(M_CHUNK, 2 * M_CHUNK))
                gate_quantise(3)
